import numpy as np
import ml_dtypes

BF16 = ml_dtypes.bfloat16


def bf(x):
    return np.asarray(x, np.float32).astype(BF16)


def f32(x):
    return np.asarray(x, np.float32)


def f64(x):
    return np.asarray(x).astype(np.float64)


def striped(idx):
    return np.tile(idx.reshape(-1, 16).T, (8, 1))


C, S, N, T, M = 256, 512, 1024, 64, 128


def pos_table():
    t = np.arange(T, dtype=np.float32)[:, None]
    div = np.exp(np.arange(0, C, 2, dtype=np.float32) * np.float32(-(np.log(10000.0) / C)))
    ang = t * div
    pe = np.zeros((T, C), np.float32)
    pe[:, 0::2] = np.sin(ang)
    pe[:, 1::2] = np.cos(ang)
    return np.tile(pe.T, (1, N // T))


def setup_inputs():
    return {"x": f32(np.random.standard_normal((C, S))), "pos": f32(pos_table()), "wv": bf(np.random.standard_normal((C, C)) / np.sqrt(C)), "bv": f32(0.1 * np.random.standard_normal((C, 1))), "wc": bf(np.random.standard_normal((C, M)) / np.sqrt(C)), "bc": f32(0.1 * np.random.standard_normal((M, 1))), "offs": striped(np.random.permutation(np.tile(np.arange(S), 2))[:N])}


def reference(x, pos, wv, bv, wc, bc, offs):
    idx = offs[:16].T.reshape(-1)
    e = f64(x)[:, idx] + f64(pos)
    v = f64(wv).T @ e + f64(bv)
    return f64(wc).T @ v + f64(bc)

@@ -1,0 +1,107 @@
+import concourse.mybir as mybir
+
+F32 = mybir.dt.float32
+BF16 = mybir.dt.bfloat16
+U16 = mybir.dt.uint16
+ADD = mybir.AluOpType.add
+IDENTITY = mybir.ActivationFunctionType.Identity
+COPY = mybir.ActivationFunctionType.Copy
+
+P = 128
+C, S, N, M = 256, 512, 1024, 128
+BLOCKS = C // P
+WIDTHS = (256, 384, 256, 128)
+STARTS = tuple(sum(WIDTHS[:t]) for t in range(len(WIDTHS)))
+PIECES = len(WIDTHS)
+LAST = PIECES - 1
+
+FLOPS = 2 * C * C * N + 2 * C * M * N
+
+
+def tile_attentionwithpositionalencoding_kernel(tc, x, pos, wv, bv, wc, bc, offs, out):
+    nc = tc.nc
+    with (
+        tc.tile_pool(name="held", bufs=1) as held,
+        tc.tile_pool(name="work", bufs=3) as work,
+        tc.psum_pool(name="v_banks", bufs=2) as v_banks,
+        tc.psum_pool(name="o_banks", bufs=4) as o_banks,
+    ):
+        offsets = held.tile([P, N // 16], U16, name="offsets")
+        table = [held.tile([P, S], F32, name=f"table{b}") for b in range(BLOCKS)]
+        place = held.tile([P, BLOCKS, N], F32, name="place")
+        wv_sb = held.tile([P, BLOCKS, C], BF16, name="wv_sb")
+        wc_sb = held.tile([P, BLOCKS, M], BF16, name="wc_sb")
+        bv_sb = held.tile([P, BLOCKS], F32, name="bv_sb")
+        bc_sb = held.tile([P, 1], F32, name="bc_sb")
+
+        def tokens(t):
+            return slice(STARTS[t], STARTS[t] + WIDTHS[t])
+
+        def load_place_block(b, cols):
+            nc.sync.dma_start(place[:, b, cols], pos[b * P : (b + 1) * P, cols])
+
+        def load_place(cols):
+            nc.sync.dma_start(place[:, :, cols], pos[:, cols].rearrange("(b p) j -> p b j", p=P))
+
+        nc.sync.dma_start(offsets[:], offs)
+        nc.sync.dma_start(table[0][:], x[0:P, :])
+        load_place_block(0, tokens(0))
+        load_place_block(0, tokens(1))
+        nc.sync.dma_start(table[1][:], x[P : 2 * P, :])
+        load_place_block(1, tokens(0))
+        nc.sync.dma_start(wv_sb[:], wv.rearrange("(b p) d -> p b d", p=P))
+        load_place_block(1, tokens(1))
+        load_place(slice(STARTS[2], N))
+        nc.sync.dma_start(bv_sb[:], bv.rearrange("(b p) o -> p (b o)", p=P))
+        nc.sync.dma_start(wc_sb[:], wc.rearrange("(b p) m -> p b m", p=P))
+        nc.sync.dma_start(bc_sb[:], bc)
+
+        v_sums = {}
+        o_sums = {}
+
+        def embed_and_project(b, t):
+            e_f32 = work.tile([P, WIDTHS[t]], F32, name=f"e_f32_{b}")
+            piece_offsets = offsets[:, STARTS[t] // 16 : (STARTS[t] + WIDTHS[t]) // 16]
+            nc.vector.tensor_tensor(e_f32[:], table[b][:].indirect(piece_offsets), place[:, b, tokens(t)], ADD)
+            e_bf = work.tile([P, WIDTHS[t]], BF16, name=f"e_bf{b}")
+            if t == LAST and b == BLOCKS - 1:
+                nc.vector.tensor_copy(e_bf[:], e_f32[:])
+            else:
+                nc.scalar.activation(e_bf[:], e_f32[:], COPY)
+            if b == 0:
+                v_sums[t] = [v_banks.tile([P, WIDTHS[t]], F32, name=f"v_ps{d}") for d in range(BLOCKS)]
+            for d in range(BLOCKS):
+                nc.tensor.matmul(
+                    v_sums[t][d][:], wv_sb[:, b, d * P : (d + 1) * P], e_bf[:], start=(b == 0), stop=(b == BLOCKS - 1)
+                )
+
+        def bias_and_classify(t):
+            o_sums[t] = o_banks.tile([P, WIDTHS[t]], F32, name="o_ps")
+            for d in range(BLOCKS):
+                v_bf = work.tile([P, WIDTHS[t]], BF16, name=f"v_bf{d}")
+                if t == LAST and d == BLOCKS - 1:
+                    nc.vector.tensor_scalar_add(v_bf[:], v_sums[t][d][:], bv_sb[:, d : d + 1])
+                else:
+                    nc.scalar.activation(v_bf[:], v_sums[t][d][:], IDENTITY, bias=bv_sb[:, d : d + 1])
+                nc.tensor.matmul(o_sums[t][:], wc_sb[:, d, :], v_bf[:], start=(d == 0), stop=(d == BLOCKS - 1))
+
+        def bias_and_store(t):
+            o_sb = held.tile([P, WIDTHS[t]], F32, name=f"o_sb{t}")
+            nc.vector.tensor_scalar_add(o_sb[:], o_sums[t][:], bc_sb[:])
+            nc.sync.dma_start(out[:, tokens(t)], o_sb[:])
+
+        embed_and_project(0, 0)
+        embed_and_project(0, 1)
+        embed_and_project(1, 0)
+        embed_and_project(1, 1)
+        bias_and_classify(0)
+        for t in range(2, PIECES):
+            for b in range(BLOCKS):
+                embed_and_project(b, t)
+            bias_and_classify(t - 1)
+
+        for t in range(2):
+            bias_and_store(t)
+        bias_and_classify(LAST)
+        for t in range(2, PIECES):
+            bias_and_store(t)

@@ -32,28 +32,30 @@ def tile_attentionwithpositionalencoding_kernel(tc, x, pos, wv, bv, wc, bc, offs
         wv_sb = held.tile([P, BLOCKS, C], BF16, name="wv_sb")
         wc_sb = held.tile([P, BLOCKS, M], BF16, name="wc_sb")
         bv_sb = held.tile([P, BLOCKS], F32, name="bv_sb")
+        x_rows = x.rearrange("(p b) s -> p b s", b=BLOCKS)
+        pos_rows = pos.rearrange("(p b) j -> p b j", b=BLOCKS)
         bc_sb = held.tile([P, 1], F32, name="bc_sb")
 
         def tokens(t):
             return slice(STARTS[t], STARTS[t] + WIDTHS[t])
 
         def load_place_block(b, cols):
-            nc.sync.dma_start(place[:, b, cols], pos[b * P : (b + 1) * P, cols])
+            nc.sync.dma_start(place[:, b, cols], pos_rows[:, b, cols])
 
         def load_place(cols):
-            nc.sync.dma_start(place[:, :, cols], pos[:, cols].rearrange("(b p) j -> p b j", p=P))
+            nc.sync.dma_start(place[:, :, cols], pos_rows[:, :, cols])
 
         nc.sync.dma_start(offsets[:], offs)
-        nc.sync.dma_start(table[0][:], x[0:P, :])
+        nc.sync.dma_start(table[0][:], x_rows[:, 0, :])
         load_place_block(0, tokens(0))
         load_place_block(0, tokens(1))
-        nc.sync.dma_start(table[1][:], x[P : 2 * P, :])
+        nc.sync.dma_start(table[1][:], x_rows[:, 1, :])
         load_place_block(1, tokens(0))
-        nc.sync.dma_start(wv_sb[:], wv.rearrange("(b p) d -> p b d", p=P))
+        nc.sync.dma_start(wv_sb[:], wv.rearrange("(p b) d -> p b d", b=BLOCKS))
         load_place_block(1, tokens(1))
         load_place(slice(STARTS[2], N))
-        nc.sync.dma_start(bv_sb[:], bv.rearrange("(b p) o -> p (b o)", p=P))
-        nc.sync.dma_start(wc_sb[:], wc.rearrange("(b p) m -> p b m", p=P))
+        nc.sync.dma_start(bv_sb[:], bv.rearrange("(p b) o -> p (b o)", b=BLOCKS))
+        nc.sync.dma_start(wc_sb[:], wc.rearrange("(p b) m -> p b m", b=BLOCKS))
         nc.sync.dma_start(bc_sb[:], bc)
 
         v_sums = {}
@@ -64,7 +66,7 @@ def tile_attentionwithpositionalencoding_kernel(tc, x, pos, wv, bv, wc, bc, offs
             piece_offsets = offsets[:, STARTS[t] // 16 : (STARTS[t] + WIDTHS[t]) // 16]
             nc.vector.tensor_tensor(e_f32[:], table[b][:].indirect(piece_offsets), place[:, b, tokens(t)], ADD)
             e_bf = work.tile([P, WIDTHS[t]], BF16, name=f"e_bf{b}")
-            if t == LAST and b == BLOCKS - 1:
+            if t >= LAST - 1 and b == BLOCKS - 1:
                 nc.vector.tensor_copy(e_bf[:], e_f32[:])
             else:
                 nc.scalar.activation(e_bf[:], e_f32[:], COPY)
@@ -72,7 +74,7 @@ def tile_attentionwithpositionalencoding_kernel(tc, x, pos, wv, bv, wc, bc, offs
                 v_sums[t] = [v_banks.tile([P, WIDTHS[t]], F32, name=f"v_ps{d}") for d in range(BLOCKS)]
             for d in range(BLOCKS):
                 nc.tensor.matmul(
-                    v_sums[t][d][:], wv_sb[:, b, d * P : (d + 1) * P], e_bf[:], start=(b == 0), stop=(b == BLOCKS - 1)
+                    v_sums[t][d][:], wv_sb[:, b, d::BLOCKS], e_bf[:], start=(b == 0), stop=(b == BLOCKS - 1)
                 )
 
         def bias_and_classify(t):

import concourse.mybir as mybir

F32 = mybir.dt.float32
BF16 = mybir.dt.bfloat16
U16 = mybir.dt.uint16
ADD = mybir.AluOpType.add
IDENTITY = mybir.ActivationFunctionType.Identity
COPY = mybir.ActivationFunctionType.Copy

P = 128
C, S, N, M = 256, 512, 1024, 128
BLOCKS = C // P
WIDTHS = (256, 384, 256, 128)
STARTS = tuple(sum(WIDTHS[:t]) for t in range(len(WIDTHS)))
PIECES = len(WIDTHS)
LAST = PIECES - 1

FLOPS = 2 * C * C * N + 2 * C * M * N


def tile_attentionwithpositionalencoding_kernel(tc, x, pos, wv, bv, wc, bc, offs, out):
    nc = tc.nc
    with (
        tc.tile_pool(name="held", bufs=1) as held,
        tc.tile_pool(name="work", bufs=3) as work,
        tc.psum_pool(name="v_banks", bufs=2) as v_banks,
        tc.psum_pool(name="o_banks", bufs=4) as o_banks,
    ):
        offsets = held.tile([P, N // 16], U16, name="offsets")
        table = [held.tile([P, S], F32, name=f"table{b}") for b in range(BLOCKS)]
        place = held.tile([P, BLOCKS, N], F32, name="place")
        wv_sb = held.tile([P, BLOCKS, C], BF16, name="wv_sb")
        wc_sb = held.tile([P, BLOCKS, M], BF16, name="wc_sb")
        bv_sb = held.tile([P, BLOCKS], F32, name="bv_sb")
        x_rows = x.rearrange("(p b) s -> p b s", b=BLOCKS)
        pos_rows = pos.rearrange("(p b) j -> p b j", b=BLOCKS)
        bc_sb = held.tile([P, 1], F32, name="bc_sb")

        def tokens(t):
            return slice(STARTS[t], STARTS[t] + WIDTHS[t])

        def load_place_block(b, cols):
            nc.sync.dma_start(place[:, b, cols], pos_rows[:, b, cols])

        def load_place(cols):
            nc.sync.dma_start(place[:, :, cols], pos_rows[:, :, cols])

        nc.sync.dma_start(offsets[:], offs)
        nc.sync.dma_start(table[0][:], x_rows[:, 0, :])
        load_place_block(0, tokens(0))
        load_place_block(0, tokens(1))
        nc.sync.dma_start(table[1][:], x_rows[:, 1, :])
        load_place_block(1, tokens(0))
        nc.sync.dma_start(wv_sb[:], wv.rearrange("(p b) d -> p b d", b=BLOCKS))
        load_place_block(1, tokens(1))
        load_place(slice(STARTS[2], N))
        nc.sync.dma_start(bv_sb[:], bv.rearrange("(p b) o -> p (b o)", b=BLOCKS))
        nc.sync.dma_start(wc_sb[:], wc.rearrange("(p b) m -> p b m", b=BLOCKS))
        nc.sync.dma_start(bc_sb[:], bc)

        v_sums = {}
        o_sums = {}

        def embed_and_project(b, t):
            e_f32 = work.tile([P, WIDTHS[t]], F32, name=f"e_f32_{b}")
            piece_offsets = offsets[:, STARTS[t] // 16 : (STARTS[t] + WIDTHS[t]) // 16]
            nc.vector.tensor_tensor(e_f32[:], table[b][:].indirect(piece_offsets), place[:, b, tokens(t)], ADD)
            e_bf = work.tile([P, WIDTHS[t]], BF16, name=f"e_bf{b}")
            if t >= LAST - 1 and b == BLOCKS - 1:
                nc.vector.tensor_copy(e_bf[:], e_f32[:])
            else:
                nc.scalar.activation(e_bf[:], e_f32[:], COPY)
            if b == 0:
                v_sums[t] = [v_banks.tile([P, WIDTHS[t]], F32, name=f"v_ps{d}") for d in range(BLOCKS)]
            for d in range(BLOCKS):
                nc.tensor.matmul(
                    v_sums[t][d][:], wv_sb[:, b, d::BLOCKS], e_bf[:], start=(b == 0), stop=(b == BLOCKS - 1)
                )

        def bias_and_classify(t):
            o_sums[t] = o_banks.tile([P, WIDTHS[t]], F32, name="o_ps")
            for d in range(BLOCKS):
                v_bf = work.tile([P, WIDTHS[t]], BF16, name=f"v_bf{d}")
                if t == LAST and d == BLOCKS - 1:
                    nc.vector.tensor_scalar_add(v_bf[:], v_sums[t][d][:], bv_sb[:, d : d + 1])
                else:
                    nc.scalar.activation(v_bf[:], v_sums[t][d][:], IDENTITY, bias=bv_sb[:, d : d + 1])
                nc.tensor.matmul(o_sums[t][:], wc_sb[:, d, :], v_bf[:], start=(d == 0), stop=(d == BLOCKS - 1))

        def bias_and_store(t):
            o_sb = held.tile([P, WIDTHS[t]], F32, name=f"o_sb{t}")
            nc.vector.tensor_scalar_add(o_sb[:], o_sums[t][:], bc_sb[:])
            nc.sync.dma_start(out[:, tokens(t)], o_sb[:])

        embed_and_project(0, 0)
        embed_and_project(0, 1)
        embed_and_project(1, 0)
        embed_and_project(1, 1)
        bias_and_classify(0)
        for t in range(2, PIECES):
            for b in range(BLOCKS):
                embed_and_project(b, t)
            bias_and_classify(t - 1)

        for t in range(2):
            bias_and_store(t)
        bias_and_classify(LAST)
        for t in range(2, PIECES):
            bias_and_store(t)
